import numpy as np
import ml_dtypes


def mxq(x, axis, fmt="e4m3"):
    dtype, down = {"e4m3": (ml_dtypes.float8_e4m3fn, 7), "e5m2": (ml_dtypes.float8_e5m2, 14)}[fmt]
    v = np.moveaxis(np.asarray(x, np.float32).astype(ml_dtypes.bfloat16).astype(np.float64), axis, -1)
    blocks = v.reshape(v.shape[:-1] + (-1, 32))
    amax = np.abs(blocks).max(-1, keepdims=True)
    byte = np.maximum(np.where(amax > 0, np.frexp(amax)[1] - 1 + 127, 0) - down, 1)
    scale = np.exp2(byte - 127.0)
    codes = (blocks / scale).astype(np.float32).astype(dtype).astype(np.float64)
    return np.moveaxis((codes * scale).reshape(v.shape), -1, axis)


WIDE = False


def mx_kscale(k):
    if not WIDE:
        return np.ones(k)
    levels = np.array([20, -20, 10, -10, 0])
    a = np.random.permutation(np.resize(levels, k // 512 * 4)).reshape(k // 512, 4)
    idx = np.arange(k)
    return np.exp2(a[idx // 512, idx % 128 // 32])


BF16 = ml_dtypes.bfloat16


def bf(x):
    return np.asarray(x, np.float32).astype(BF16)


def f64(x):
    return np.asarray(x).astype(np.float64)


N, IN, OUT = 1024, 2048, 2048


def setup_inputs():
    u = mx_kscale(OUT)
    x = np.random.standard_normal((N, IN))
    weight = np.random.standard_normal((OUT, IN)) * 0.02 / u[:, None]
    bias = np.random.standard_normal(OUT) * 0.5
    input_scale = np.ones(1)
    g = np.random.standard_normal((N, OUT)) * np.exp2(np.random.randint(-12, 1, (N, 1))) * 8.0 * u[None, :]
    return {"x": bf(x), "weight": bf(weight), "bias": bf(bias),
            "input_scale": bf(input_scale), "grad_out": bf(g)}


def reference(x, weight, bias, input_scale, grad_out):
    gq = mxq(f64(grad_out), 1, "e5m2")
    wq = mxq(f64(weight), 0, "e4m3")
    return gq @ wq

@@ -1,0 +1,170 @@
+from contextlib import ExitStack
+
+import concourse.mybir as mybir
+from concourse.masks import make_identity
+
+F32 = mybir.dt.float32
+BF16 = mybir.dt.bfloat16
+U32 = mybir.dt.uint32
+U8 = mybir.dt.uint8
+E4X4 = mybir.dt.float8_e4m3fn_x4
+E5X4 = mybir.dt.float8_e5m2_x4
+
+P = 128
+TOK = 1024
+K = 2048
+IN = 2048
+A = TOK // P
+C = K // 512
+NT = 512
+NN = IN // NT
+
+FLOPS = 2 * TOK * K * IN
+BYTES = 2 * (TOK * K + K * IN) + 4 * TOK * IN
+
+V_COLS = 320
+
+
+def tile_inputscaledquantlinear_kernel(tc, x, weight, bias, input_scale, grad_out, out):
+    nc = tc.nc
+    g_view = grad_out.rearrange("(p a) k -> p a k", a=A)
+    o_view = out.rearrange("(p a) n -> p a n", a=A)
+
+    with ExitStack() as ctx:
+        const = ctx.enter_context(tc.tile_pool(name="const", bufs=1))
+        big = ctx.enter_context(tc.tile_pool(name="big", bufs=8))
+        wraw = ctx.enter_context(tc.tile_pool(name="wraw", bufs=1))
+        keep = ctx.enter_context(tc.tile_pool(name="keep", bufs=1))
+        ggrp = ctx.enter_context(tc.tile_pool(name="ggrp", bufs=3))
+        wgrp = ctx.enter_context(tc.tile_pool(name="wgrp", bufs=4))
+        psum = ctx.enter_context(tc.psum_pool(name="psum", bufs=1))
+
+        ident = const.tile([P, P], F32, name="ident")
+        make_identity(nc, ident[:])
+
+        g_raw = []
+        for j in range(A // 2):
+            t = big.tile([P, 2, K], BF16, name="graw%d" % j, tag="big")
+            nc.sync.dma_start(out=t[:], in_=g_view[:, 2 * j : 2 * j + 2, :])
+            g_raw.append(t)
+
+        w_src = {}
+
+        def load_w(c, col0, width, name):
+            t = wraw.tile([P, 4, width], BF16, name=name)
+            for u in range(2):
+                r0 = 512 * c + 256 * u
+                nc.sync.dma_start(
+                    out=t[:, 2 * u : 2 * u + 2, :],
+                    in_=weight[r0 : r0 + 256, col0 : col0 + width].rearrange("(q e) w -> q e w", e=2),
+                )
+            return t
+
+        for n in range(2):
+            for c in range(C):
+                t = load_w(c, NT * n, NT, "wr%d_%d" % (c, n))
+                w_src[(c, n)] = t[:, :, :]
+        for c in range(C):
+            t = load_w(c, 2 * NT, 2 * NT, "wrb%d" % c)
+            w_src[(c, 2)] = t[:, :, 0:NT]
+            w_src[(c, 3)] = t[:, :, NT : 2 * NT]
+
+        g_codes = []
+        g_scales = []
+        for a in range(A):
+            words = g_raw[a // 2][:, a % 2, :].bitcast(F32)
+            grp = ggrp.tile([P, C, P, 2], F32, name="ggrp", align_bytes=64)
+            for b in range(2):
+                bank = (2 * a + b) % 8
+                xt = psum.tile([P, 2, 2, P], F32, name="xt%d_%d" % (a, b), tag="bank%d" % bank)
+                for c2 in range(2):
+                    for u in range(2):
+                        w0 = 256 * (2 * b + c2) + 128 * u
+                        nc.tensor.transpose(xt[:, c2, u, :], words[:, w0 : w0 + 128], ident[:])
+                src = xt[:].rearrange("p c u r -> p c r u")
+                dst = grp[:, 2 * b : 2 * b + 2, :, :]
+                if b == 1 and a % 2 == 1:
+                    nc.vector.tensor_copy(out=dst, in_=src)
+                else:
+                    nc.scalar.copy(out=dst, in_=src)
+            gc = keep.tile([P, C * P], U32, name="gc%d" % a, align_bytes=64)
+            gs = keep.tile([P, C * P], U8, name="gs%d" % a, align_bytes=64)
+            nc.vector.quantize_mx(
+                out=gc[:].bitcast(E5X4),
+                scales=gs[:],
+                in_=grp[:].rearrange("p c r u -> p (c r u)").bitcast(BF16),
+            )
+            g_codes.append(gc)
+            g_scales.append(gs)
+
+        w_codes = {}
+        w_scales = {}
+
+        def prep_w(c, n):
+            src = w_src[(c, n)]
+            grp = wgrp.tile([P, NT, 4], BF16, name="wgrp", align_bytes=64)
+            nc.vector.tensor_copy(
+                out=grp[:, 0:V_COLS, :].rearrange("p (c i) t -> p c t i", i=4),
+                in_=src[:, :, 0:V_COLS].rearrange("p t (c i) -> p c t i", i=4),
+            )
+            nc.scalar.copy(
+                out=grp[:, V_COLS:NT, :].rearrange("p (c i) t -> p c t i", i=4),
+                in_=src[:, :, V_COLS:NT].rearrange("p t (c i) -> p c t i", i=4),
+            )
+            wc = keep.tile([P, NT], U32, name="wc%d_%d" % (c, n), align_bytes=64)
+            ws = keep.tile([P, NT], U8, name="ws%d_%d" % (c, n), align_bytes=64)
+            nc.vector.quantize_mx(
+                out=wc[:].bitcast(E4X4),
+                scales=ws[:],
+                in_=grp[:].rearrange("p w t -> p (w t)"),
+            )
+            w_codes[(c, n)] = wc
+            w_scales[(c, n)] = ws
+
+        out_rows = {}
+        count = [0]
+
+        def run_set(groups):
+            accs = []
+            for a, n in groups:
+                bank = count[0] % 8
+                accs.append(psum.tile([P, NT], F32, name="acc%d_%d" % (a, n), tag="bank%d" % bank))
+                count[0] += 1
+            for c in range(C):
+                for (a, n), acc in zip(groups, accs):
+                    nc.tensor.matmul_mx(
+                        out=acc[:],
+                        lhsT=g_codes[a][:, P * c : P * c + P].bitcast(E5X4),
+                        lhsT_scale=g_scales[a][:, P * c : P * c + P],
+                        rhs=w_codes[(c, n)][:].bitcast(E4X4),
+                        rhs_scale=w_scales[(c, n)][:],
+                        start=(c == 0),
+                        stop=(c == C - 1),
+                    )
+            for i, ((a, n), acc) in enumerate(zip(groups, accs)):
+                if a not in out_rows:
+                    out_rows[a] = big.tile([P, IN], F32, name="orow%d" % a, tag="big")
+                dst = out_rows[a][:, NT * n : NT * n + NT]
+                if (a + n) % 4 == 3:
+                    nc.vector.tensor_copy(out=dst, in_=acc[:])
+                else:
+                    nc.scalar.copy(out=dst, in_=acc[:])
+                if n % 2 == 1:
+                    lo = NT * (n - 1)
+                    nc.sync.dma_start(out=o_view[:, a, lo : lo + 2 * NT], in_=out_rows[a][:, lo : lo + 2 * NT])
+
+        for c in range(C):
+            prep_w(c, 0)
+        run_set([(a, 0) for a in range(A)])
+        for c in range(C):
+            prep_w(c, 1)
+        run_set([(a, 1) for a in range(0, 4)])
+        run_set([(a, 1) for a in range(4, 8)])
+        for c in range(C):
+            prep_w(c, 2)
+        run_set([(a, 2) for a in range(0, 4)])
+        for c in range(C):
+            prep_w(c, 3)
+        run_set([(a, 2) for a in range(4, 8)])
+        for a in range(A):
+            run_set([(a, 3)])

@@ -17,12 +17,11 @@ IN = 2048
 A = TOK // P
 C = K // 512
 NT = 512
-NN = IN // NT
 
 FLOPS = 2 * TOK * K * IN
 BYTES = 2 * (TOK * K + K * IN) + 4 * TOK * IN
 
-V_COLS = 320
+V_COLS = 352
 
 
 def tile_inputscaledquantlinear_kernel(tc, x, weight, bias, input_scale, grad_out, out):
@@ -38,133 +37,185 @@ def tile_inputscaledquantlinear_kernel(tc, x, weight, bias, input_scale, grad_ou
         ggrp = ctx.enter_context(tc.tile_pool(name="ggrp", bufs=3))
         wgrp = ctx.enter_context(tc.tile_pool(name="wgrp", bufs=4))
         psum = ctx.enter_context(tc.psum_pool(name="psum", bufs=1))
+        ctx.enter_context(tc.manual_schedule())
 
         ident = const.tile([P, P], F32, name="ident")
         make_identity(nc, ident[:])
 
-        g_raw = []
-        for j in range(A // 2):
-            t = big.tile([P, 2, K], BF16, name="graw%d" % j, tag="big")
-            nc.sync.dma_start(out=t[:], in_=g_view[:, 2 * j : 2 * j + 2, :])
-            g_raw.append(t)
-
+        g_words = {}
         w_src = {}
 
-        def load_w(c, col0, width, name):
-            t = wraw.tile([P, 4, width], BF16, name=name)
+        def load_g(j, parts):
+            t = big.tile([P, 2, K], BF16, name="graw%d" % j, tag="big")
+            for lo, hi in parts:
+                nc.sync.dma_start(out=t[:, lo:hi, :], in_=g_view[:, 2 * j + lo : 2 * j + hi, :])
+            for i in range(2):
+                g_words[2 * j + i] = t[:, i, :].bitcast(F32)
+
+        def load_w(c, n0, nn):
+            t = wraw.tile([P, 4, NT * nn], BF16, name="wr%d_%d" % (c, n0))
             for u in range(2):
                 r0 = 512 * c + 256 * u
                 nc.sync.dma_start(
                     out=t[:, 2 * u : 2 * u + 2, :],
-                    in_=weight[r0 : r0 + 256, col0 : col0 + width].rearrange("(q e) w -> q e w", e=2),
+                    in_=weight[r0 : r0 + 256, NT * n0 : NT * (n0 + nn)].rearrange("(q e) w -> q e w", e=2),
                 )
-            return t
+            for i in range(nn):
+                w_src[(c, n0 + i)] = t[:, :, NT * i : NT * (i + 1)]
 
-        for n in range(2):
-            for c in range(C):
-                t = load_w(c, NT * n, NT, "wr%d_%d" % (c, n))
-                w_src[(c, n)] = t[:, :, :]
+        for j in range(3):
+            load_g(j, [(0, 2)])
+        load_w(0, 0, 1)
+        load_g(3, [(0, 1), (1, 2)])
+        for c in range(1, C):
+            load_w(c, 0, 1)
         for c in range(C):
-            t = load_w(c, 2 * NT, 2 * NT, "wrb%d" % c)
-            w_src[(c, 2)] = t[:, :, 0:NT]
-            w_src[(c, 3)] = t[:, :, NT : 2 * NT]
+            load_w(c, 1, 1)
+        for c in range(C):
+            load_w(c, 2, 2)
 
-        g_codes = []
-        g_scales = []
-        for a in range(A):
-            words = g_raw[a // 2][:, a % 2, :].bitcast(F32)
+        g_grp = {}
+        g_codes = {}
+        g_scales = {}
+
+        def g_transpose(a, vector_second):
             grp = ggrp.tile([P, C, P, 2], F32, name="ggrp", align_bytes=64)
+            g_grp[a] = grp
             for b in range(2):
                 bank = (2 * a + b) % 8
                 xt = psum.tile([P, 2, 2, P], F32, name="xt%d_%d" % (a, b), tag="bank%d" % bank)
                 for c2 in range(2):
                     for u in range(2):
                         w0 = 256 * (2 * b + c2) + 128 * u
-                        nc.tensor.transpose(xt[:, c2, u, :], words[:, w0 : w0 + 128], ident[:])
+                        nc.tensor.transpose(xt[:, c2, u, :], g_words[a][:, w0 : w0 + 128], ident[:])
                 src = xt[:].rearrange("p c u r -> p c r u")
                 dst = grp[:, 2 * b : 2 * b + 2, :, :]
-                if b == 1 and a % 2 == 1:
+                if b == 1 and vector_second:
                     nc.vector.tensor_copy(out=dst, in_=src)
                 else:
                     nc.scalar.copy(out=dst, in_=src)
+
+        def g_quantise(a):
             gc = keep.tile([P, C * P], U32, name="gc%d" % a, align_bytes=64)
             gs = keep.tile([P, C * P], U8, name="gs%d" % a, align_bytes=64)
             nc.vector.quantize_mx(
                 out=gc[:].bitcast(E5X4),
                 scales=gs[:],
-                in_=grp[:].rearrange("p c r u -> p (c r u)").bitcast(BF16),
+                in_=g_grp[a][:].rearrange("p c r u -> p (c r u)").bitcast(BF16),
             )
-            g_codes.append(gc)
-            g_scales.append(gs)
+            g_codes[a] = gc
+            g_scales[a] = gs
 
+        w_grp = {}
         w_codes = {}
         w_scales = {}
 
-        def prep_w(c, n):
+        def w_regroup(c, n, v_cols):
             src = w_src[(c, n)]
             grp = wgrp.tile([P, NT, 4], BF16, name="wgrp", align_bytes=64)
+            w_grp[(c, n)] = grp
             nc.vector.tensor_copy(
-                out=grp[:, 0:V_COLS, :].rearrange("p (c i) t -> p c t i", i=4),
-                in_=src[:, :, 0:V_COLS].rearrange("p t (c i) -> p c t i", i=4),
+                out=grp[:, 0:v_cols, :].rearrange("p (c i) t -> p c t i", i=4),
+                in_=src[:, :, 0:v_cols].rearrange("p t (c i) -> p c t i", i=4),
             )
-            nc.scalar.copy(
-                out=grp[:, V_COLS:NT, :].rearrange("p (c i) t -> p c t i", i=4),
-                in_=src[:, :, V_COLS:NT].rearrange("p t (c i) -> p c t i", i=4),
-            )
+            if v_cols < NT:
+                nc.scalar.copy(
+                    out=grp[:, v_cols:NT, :].rearrange("p (c i) t -> p c t i", i=4),
+                    in_=src[:, :, v_cols:NT].rearrange("p t (c i) -> p c t i", i=4),
+                )
+
+        def w_quantise(c, n):
             wc = keep.tile([P, NT], U32, name="wc%d_%d" % (c, n), align_bytes=64)
             ws = keep.tile([P, NT], U8, name="ws%d_%d" % (c, n), align_bytes=64)
             nc.vector.quantize_mx(
                 out=wc[:].bitcast(E4X4),
                 scales=ws[:],
-                in_=grp[:].rearrange("p w t -> p (w t)"),
+                in_=w_grp[(c, n)][:].rearrange("p w t -> p (w t)"),
             )
             w_codes[(c, n)] = wc
             w_scales[(c, n)] = ws
 
+        accs = {}
         out_rows = {}
-        count = [0]
 
-        def run_set(groups):
-            accs = []
-            for a, n in groups:
-                bank = count[0] % 8
-                accs.append(psum.tile([P, NT], F32, name="acc%d_%d" % (a, n), tag="bank%d" % bank))
-                count[0] += 1
-            for c in range(C):
-                for (a, n), acc in zip(groups, accs):
-                    nc.tensor.matmul_mx(
-                        out=acc[:],
-                        lhsT=g_codes[a][:, P * c : P * c + P].bitcast(E5X4),
-                        lhsT_scale=g_scales[a][:, P * c : P * c + P],
-                        rhs=w_codes[(c, n)][:].bitcast(E4X4),
-                        rhs_scale=w_scales[(c, n)][:],
-                        start=(c == 0),
-                        stop=(c == C - 1),
-                    )
-            for i, ((a, n), acc) in enumerate(zip(groups, accs)):
-                if a not in out_rows:
-                    out_rows[a] = big.tile([P, IN], F32, name="orow%d" % a, tag="big")
-                dst = out_rows[a][:, NT * n : NT * n + NT]
-                if (a + n) % 4 == 3:
-                    nc.vector.tensor_copy(out=dst, in_=acc[:])
-                else:
-                    nc.scalar.copy(out=dst, in_=acc[:])
-                if n % 2 == 1:
-                    lo = NT * (n - 1)
-                    nc.sync.dma_start(out=o_view[:, a, lo : lo + 2 * NT], in_=out_rows[a][:, lo : lo + 2 * NT])
+        def sweep(tiles, n, c):
+            for a in tiles:
+                if c == 0:
+                    accs[(a, n)] = psum.tile([P, NT], F32, name="acc%d_%d" % (a, n), tag="bank%d" % a)
+                nc.tensor.matmul_mx(
+                    out=accs[(a, n)][:],
+                    lhsT=g_codes[a][:, P * c : P * c + P].bitcast(E5X4),
+                    lhsT_scale=g_scales[a][:, P * c : P * c + P],
+                    rhs=w_codes[(c, n)][:].bitcast(E4X4),
+                    rhs_scale=w_scales[(c, n)][:],
+                    start=(c == 0),
+                    stop=(c == C - 1),
+                )
 
-        for c in range(C):
-            prep_w(c, 0)
-        run_set([(a, 0) for a in range(A)])
-        for c in range(C):
-            prep_w(c, 1)
-        run_set([(a, 1) for a in range(0, 4)])
-        run_set([(a, 1) for a in range(4, 8)])
-        for c in range(C):
-            prep_w(c, 2)
-        run_set([(a, 2) for a in range(0, 4)])
-        for c in range(C):
-            prep_w(c, 3)
-        run_set([(a, 2) for a in range(4, 8)])
+        def evacuate(a, n, lo=0, hi=NT):
+            if a not in out_rows:
+                out_rows[a] = big.tile([P, IN], F32, name="orow%d" % a, tag="big")
+            nc.scalar.copy(out=out_rows[a][:, NT * n + lo : NT * n + hi], in_=accs[(a, n)][:, lo:hi])
+
+        def store(a, lo, hi):
+            nc.sync.dma_start(out=o_view[:, a, lo:hi], in_=out_rows[a][:, lo:hi])
+
+        low = [0, 1, 2, 3]
+        high = [4, 5, 6, 7]
+
+        for a in range(6):
+            g_transpose(a, a % 2 == 1)
+            g_quantise(a)
+        w_regroup(0, 0, NT)
+        g_transpose(6, False)
+        w_quantise(0, 0)
+        g_transpose(7, False)
+        g_quantise(6)
+        w_regroup(1, 0, V_COLS)
+        g_quantise(7)
+        w_quantise(1, 0)
+
+        sweep(low + high, 0, 0)
+        w_regroup(2, 0, V_COLS)
+        w_quantise(2, 0)
+        sweep(low + high, 0, 1)
+        w_regroup(3, 0, V_COLS)
+        w_quantise(3, 0)
+        sweep(low, 0, 2)
+        sweep(low, 0, 3)
+        w_regroup(0, 1, V_COLS)
+        w_quantise(0, 1)
+        w_regroup(1, 1, V_COLS)
+        w_quantise(1, 1)
+        for a in low:
+            evacuate(a, 0)
+        sweep(high, 0, 2)
+        sweep(high, 0, 3)
+        for a in high:
+            evacuate(a, 0)
+
+        rest = [(2, 1), (3, 1), (0, 2), (0, 3), (1, 2), (2, 2), (3, 2), (1, 3), (2, 3), (3, 3)]
+        for i, (c, n) in enumerate(rest):
+            w_regroup(c, n, NT)
+            if i > 0:
+                w_quantise(rest[i - 1][0], rest[i - 1][1])
+        w_quantise(3, 3)
+
+        for n in (1, 2):
+            for tiles in (low, high):
+                for c in range(C):
+                    sweep(tiles, n, c)
+                for a in tiles:
+                    evacuate(a, n)
+                    if n == 1:
+                        store(a, 0, 2 * NT)
+        store(7, 2 * NT, 3 * NT)
         for a in range(A):
-            run_set([(a, 3)])
+            for c in range(C):
+                sweep([a], 3, c)
+            if a < A - 1:
+                evacuate(a, 3)
+                store(a, 2 * NT, 4 * NT)
+        for lo in (0, NT // 2):
+            evacuate(7, 3, lo, lo + NT // 2)
+            store(7, 3 * NT + lo, 3 * NT + lo + NT // 2)

@@ -39,8 +39,18 @@ def tile_inputscaledquantlinear_kernel(tc, x, weight, bias, input_scale, grad_ou
         psum = ctx.enter_context(tc.psum_pool(name="psum", bufs=1))
         ctx.enter_context(tc.manual_schedule())
 
+        zeros = const.tile([P, NT], BF16, name="zeros")
+        nc.vector.memset(zeros[:], 0.0)
         ident = const.tile([P, P], F32, name="ident")
         make_identity(nc, ident[:])
+
+        warm = psum.tile([P, NT], F32, name="warm", tag="bank0")
+
+        def dummy(times):
+            for i in range(times):
+                nc.tensor.matmul(out=warm[:], lhsT=zeros[:, 0:P], rhs=zeros[:], start=True, stop=True)
+
+        dummy(10)
 
         g_words = {}
         w_src = {}
@@ -82,7 +92,7 @@ def tile_inputscaledquantlinear_kernel(tc, x, weight, bias, input_scale, grad_ou
             grp = ggrp.tile([P, C, P, 2], F32, name="ggrp", align_bytes=64)
             g_grp[a] = grp
             for b in range(2):
-                bank = (2 * a + b) % 8
+                bank = 2 + (2 * a + b) % 6
                 xt = psum.tile([P, 2, 2, P], F32, name="xt%d_%d" % (a, b), tag="bank%d" % bank)
                 for c2 in range(2):
                     for u in range(2):
@@ -94,6 +104,8 @@ def tile_inputscaledquantlinear_kernel(tc, x, weight, bias, input_scale, grad_ou
                     nc.vector.tensor_copy(out=dst, in_=src)
                 else:
                     nc.scalar.copy(out=dst, in_=src)
+            if a < A - 1:
+                dummy(1)
 
         def g_quantise(a):
             gc = keep.tile([P, C * P], U32, name="gc%d" % a, align_bytes=64)

@@ -35,7 +35,7 @@ def tile_inputscaledquantlinear_kernel(tc, x, weight, bias, input_scale, grad_ou
         wraw = ctx.enter_context(tc.tile_pool(name="wraw", bufs=1))
         keep = ctx.enter_context(tc.tile_pool(name="keep", bufs=1))
         ggrp = ctx.enter_context(tc.tile_pool(name="ggrp", bufs=3))
-        wgrp = ctx.enter_context(tc.tile_pool(name="wgrp", bufs=4))
+        wgrp = ctx.enter_context(tc.tile_pool(name="wgrp", bufs=6))
         psum = ctx.enter_context(tc.psum_pool(name="psum", bufs=1))
         ctx.enter_context(tc.manual_schedule())
 
@@ -55,12 +55,11 @@ def tile_inputscaledquantlinear_kernel(tc, x, weight, bias, input_scale, grad_ou
         g_words = {}
         w_src = {}
 
-        def load_g(j, parts):
-            t = big.tile([P, 2, K], BF16, name="graw%d" % j, tag="big")
-            for lo, hi in parts:
-                nc.sync.dma_start(out=t[:, lo:hi, :], in_=g_view[:, 2 * j + lo : 2 * j + hi, :])
-            for i in range(2):
-                g_words[2 * j + i] = t[:, i, :].bitcast(F32)
+        def load_g(a0, count):
+            t = big.tile([P, count, K], BF16, name="graw%d" % a0, tag="big")
+            nc.sync.dma_start(out=t[:], in_=g_view[:, a0 : a0 + count, :])
+            for i in range(count):
+                g_words[a0 + i] = t[:, i, :].bitcast(F32)
 
         def load_w(c, n0, nn):
             t = wraw.tile([P, 4, NT * nn], BF16, name="wr%d_%d" % (c, n0))
@@ -73,10 +72,11 @@ def tile_inputscaledquantlinear_kernel(tc, x, weight, bias, input_scale, grad_ou
             for i in range(nn):
                 w_src[(c, n0 + i)] = t[:, :, NT * i : NT * (i + 1)]
 
-        for j in range(3):
-            load_g(j, [(0, 2)])
         load_w(0, 0, 1)
-        load_g(3, [(0, 1), (1, 2)])
+        load_g(0, 2)
+        load_g(2, 2)
+        for a in range(4, A):
+            load_g(a, 1)
         for c in range(1, C):
             load_w(c, 0, 1)
         for c in range(C):
@@ -104,7 +104,7 @@ def tile_inputscaledquantlinear_kernel(tc, x, weight, bias, input_scale, grad_ou
                     nc.vector.tensor_copy(out=dst, in_=src)
                 else:
                     nc.scalar.copy(out=dst, in_=src)
-            if a < A - 1:
+            if a < 5:
                 dummy(1)
 
         def g_quantise(a):
@@ -126,10 +126,11 @@ def tile_inputscaledquantlinear_kernel(tc, x, weight, bias, input_scale, grad_ou
             src = w_src[(c, n)]
             grp = wgrp.tile([P, NT, 4], BF16, name="wgrp", align_bytes=64)
             w_grp[(c, n)] = grp
-            nc.vector.tensor_copy(
-                out=grp[:, 0:v_cols, :].rearrange("p (c i) t -> p c t i", i=4),
-                in_=src[:, :, 0:v_cols].rearrange("p t (c i) -> p c t i", i=4),
-            )
+            if v_cols > 0:
+                nc.vector.tensor_copy(
+                    out=grp[:, 0:v_cols, :].rearrange("p (c i) t -> p c t i", i=4),
+                    in_=src[:, :, 0:v_cols].rearrange("p t (c i) -> p c t i", i=4),
+                )
             if v_cols < NT:
                 nc.scalar.copy(
                     out=grp[:, v_cols:NT, :].rearrange("p (c i) t -> p c t i", i=4),
@@ -175,59 +176,66 @@ def tile_inputscaledquantlinear_kernel(tc, x, weight, bias, input_scale, grad_ou
         low = [0, 1, 2, 3]
         high = [4, 5, 6, 7]
 
+        def round_of(n):
+            sweep(low + high, n, 0)
+            sweep(low + high, n, 1)
+            for tiles in (low, high):
+                sweep(tiles, n, 2)
+                sweep(tiles, n, 3)
+                for a in tiles:
+                    evacuate(a, n)
+                    if n == 1:
+                        store(a, 0, 2 * NT)
+                    if n == 2:
+                        store(a, 2 * NT, 3 * NT)
+
+        w_regroup(0, 0, V_COLS)
+        w_quantise(0, 0)
         for a in range(6):
             g_transpose(a, a % 2 == 1)
             g_quantise(a)
-        w_regroup(0, 0, NT)
         g_transpose(6, False)
-        w_quantise(0, 0)
         g_transpose(7, False)
         g_quantise(6)
         w_regroup(1, 0, V_COLS)
         g_quantise(7)
         w_quantise(1, 0)
+        for c, n in ((2, 0), (3, 0), (0, 1), (1, 1)):
+            w_regroup(c, n, V_COLS)
+            w_quantise(c, n)
 
-        sweep(low + high, 0, 0)
-        w_regroup(2, 0, V_COLS)
-        w_quantise(2, 0)
-        sweep(low + high, 0, 1)
-        w_regroup(3, 0, V_COLS)
-        w_quantise(3, 0)
-        sweep(low, 0, 2)
-        sweep(low, 0, 3)
-        w_regroup(0, 1, V_COLS)
-        w_quantise(0, 1)
-        w_regroup(1, 1, V_COLS)
-        w_quantise(1, 1)
-        for a in low:
-            evacuate(a, 0)
-        sweep(high, 0, 2)
-        sweep(high, 0, 3)
-        for a in high:
-            evacuate(a, 0)
+        round_of(0)
 
-        rest = [(2, 1), (3, 1), (0, 2), (0, 3), (1, 2), (2, 2), (3, 2), (1, 3), (2, 3), (3, 3)]
-        for i, (c, n) in enumerate(rest):
-            w_regroup(c, n, NT)
-            if i > 0:
-                w_quantise(rest[i - 1][0], rest[i - 1][1])
+        w_regroup(2, 1, NT)
+        w_regroup(3, 1, NT)
+        w_quantise(2, 1)
+        w_quantise(3, 1)
+        w_regroup(0, 3, 0)
+        w_regroup(1, 3, 0)
+        w_regroup(0, 2, NT)
+        w_regroup(1, 2, NT)
+        w_quantise(0, 2)
+        w_quantise(0, 3)
+        w_regroup(2, 2, NT)
+        w_quantise(1, 2)
+        w_quantise(1, 3)
+        w_regroup(3, 2, NT)
+        w_quantise(2, 2)
+        w_quantise(3, 2)
+        w_regroup(2, 3, NT)
+        w_regroup(3, 3, NT)
+        w_quantise(2, 3)
         w_quantise(3, 3)
 
-        for n in (1, 2):
-            for tiles in (low, high):
-                for c in range(C):
-                    sweep(tiles, n, c)
-                for a in tiles:
-                    evacuate(a, n)
-                    if n == 1:
-                        store(a, 0, 2 * NT)
-        store(7, 2 * NT, 3 * NT)
+        round_of(1)
+        round_of(2)
+
         for a in range(A):
             for c in range(C):
                 sweep([a], 3, c)
             if a < A - 1:
                 evacuate(a, 3)
-                store(a, 2 * NT, 4 * NT)
+                store(a, 3 * NT, 4 * NT)
         for lo in (0, NT // 2):
             evacuate(7, 3, lo, lo + NT // 2)
             store(7, 3 * NT + lo, 3 * NT + lo + NT // 2)

@@ -21,6 +21,7 @@ NT = 512
 FLOPS = 2 * TOK * K * IN
 BYTES = 2 * (TOK * K + K * IN) + 4 * TOK * IN
 
+PAD = 48
 V_COLS = 352
 
 
@@ -108,10 +109,10 @@ def tile_inputscaledquantlinear_kernel(tc, x, weight, bias, input_scale, grad_ou
                 dummy(1)
 
         def g_quantise(a):
-            gc = keep.tile([P, C * P], U32, name="gc%d" % a, align_bytes=64)
-            gs = keep.tile([P, C * P], U8, name="gs%d" % a, align_bytes=64)
+            gc = keep.tile([P, PAD + C * P], U32, name="gc%d" % a, align_bytes=256)
+            gs = keep.tile([P, C * P], U8, name="gs%d" % a, align_bytes=256)
             nc.vector.quantize_mx(
-                out=gc[:].bitcast(E5X4),
+                out=gc[:, PAD : PAD + C * P].bitcast(E5X4),
                 scales=gs[:],
                 in_=g_grp[a][:].rearrange("p c r u -> p (c r u)").bitcast(BF16),
             )
@@ -138,8 +139,8 @@ def tile_inputscaledquantlinear_kernel(tc, x, weight, bias, input_scale, grad_ou
                 )
 
         def w_quantise(c, n):
-            wc = keep.tile([P, NT], U32, name="wc%d_%d" % (c, n), align_bytes=64)
-            ws = keep.tile([P, NT], U8, name="ws%d_%d" % (c, n), align_bytes=64)
+            wc = keep.tile([P, NT], U32, name="wc%d_%d" % (c, n), align_bytes=256)
+            ws = keep.tile([P, NT], U8, name="ws%d_%d" % (c, n), align_bytes=256)
             nc.vector.quantize_mx(
                 out=wc[:].bitcast(E4X4),
                 scales=ws[:],
@@ -157,7 +158,7 @@ def tile_inputscaledquantlinear_kernel(tc, x, weight, bias, input_scale, grad_ou
                     accs[(a, n)] = psum.tile([P, NT], F32, name="acc%d_%d" % (a, n), tag="bank%d" % a)
                 nc.tensor.matmul_mx(
                     out=accs[(a, n)][:],
-                    lhsT=g_codes[a][:, P * c : P * c + P].bitcast(E5X4),
+                    lhsT=g_codes[a][:, PAD + P * c : PAD + P * c + P].bitcast(E5X4),
                     lhsT_scale=g_scales[a][:, P * c : P * c + P],
                     rhs=w_codes[(c, n)][:].bitcast(E4X4),
                     rhs_scale=w_scales[(c, n)][:],

@@ -21,7 +21,6 @@ NT = 512
 FLOPS = 2 * TOK * K * IN
 BYTES = 2 * (TOK * K + K * IN) + 4 * TOK * IN
 
-PAD = 48
 V_COLS = 352
 
 
@@ -40,18 +39,8 @@ def tile_inputscaledquantlinear_kernel(tc, x, weight, bias, input_scale, grad_ou
         psum = ctx.enter_context(tc.psum_pool(name="psum", bufs=1))
         ctx.enter_context(tc.manual_schedule())
 
-        zeros = const.tile([P, NT], BF16, name="zeros")
-        nc.vector.memset(zeros[:], 0.0)
         ident = const.tile([P, P], F32, name="ident")
         make_identity(nc, ident[:])
-
-        warm = psum.tile([P, NT], F32, name="warm", tag="bank0")
-
-        def dummy(times):
-            for i in range(times):
-                nc.tensor.matmul(out=warm[:], lhsT=zeros[:, 0:P], rhs=zeros[:], start=True, stop=True)
-
-        dummy(10)
 
         g_words = {}
         w_src = {}
@@ -105,14 +94,12 @@ def tile_inputscaledquantlinear_kernel(tc, x, weight, bias, input_scale, grad_ou
                     nc.vector.tensor_copy(out=dst, in_=src)
                 else:
                     nc.scalar.copy(out=dst, in_=src)
-            if a < 5:
-                dummy(1)
 
         def g_quantise(a):
-            gc = keep.tile([P, PAD + C * P], U32, name="gc%d" % a, align_bytes=256)
-            gs = keep.tile([P, C * P], U8, name="gs%d" % a, align_bytes=256)
+            gc = keep.tile([P, C * P], U32, name="gc%d" % a, align_bytes=64)
+            gs = keep.tile([P, C * P], U8, name="gs%d" % a, align_bytes=64)
             nc.vector.quantize_mx(
-                out=gc[:, PAD : PAD + C * P].bitcast(E5X4),
+                out=gc[:].bitcast(E5X4),
                 scales=gs[:],
                 in_=g_grp[a][:].rearrange("p c r u -> p (c r u)").bitcast(BF16),
             )
@@ -139,8 +126,8 @@ def tile_inputscaledquantlinear_kernel(tc, x, weight, bias, input_scale, grad_ou
                 )
 
         def w_quantise(c, n):
-            wc = keep.tile([P, NT], U32, name="wc%d_%d" % (c, n), align_bytes=256)
-            ws = keep.tile([P, NT], U8, name="ws%d_%d" % (c, n), align_bytes=256)
+            wc = keep.tile([P, NT], U32, name="wc%d_%d" % (c, n), align_bytes=64)
+            ws = keep.tile([P, NT], U8, name="ws%d_%d" % (c, n), align_bytes=64)
             nc.vector.quantize_mx(
                 out=wc[:].bitcast(E4X4),
                 scales=ws[:],
@@ -158,7 +145,7 @@ def tile_inputscaledquantlinear_kernel(tc, x, weight, bias, input_scale, grad_ou
                     accs[(a, n)] = psum.tile([P, NT], F32, name="acc%d_%d" % (a, n), tag="bank%d" % a)
                 nc.tensor.matmul_mx(
                     out=accs[(a, n)][:],
-                    lhsT=g_codes[a][:, PAD + P * c : PAD + P * c + P].bitcast(E5X4),
+                    lhsT=g_codes[a][:, P * c : P * c + P].bitcast(E5X4),
                     lhsT_scale=g_scales[a][:, P * c : P * c + P],
                     rhs=w_codes[(c, n)][:].bitcast(E4X4),
                     rhs_scale=w_scales[(c, n)][:],

from contextlib import ExitStack

import concourse.mybir as mybir
from concourse.masks import make_identity

F32 = mybir.dt.float32
BF16 = mybir.dt.bfloat16
U32 = mybir.dt.uint32
U8 = mybir.dt.uint8
E4X4 = mybir.dt.float8_e4m3fn_x4
E5X4 = mybir.dt.float8_e5m2_x4

P = 128
TOK = 1024
K = 2048
IN = 2048
A = TOK // P
C = K // 512
NT = 512

FLOPS = 2 * TOK * K * IN
BYTES = 2 * (TOK * K + K * IN) + 4 * TOK * IN

V_COLS = 352


def tile_inputscaledquantlinear_kernel(tc, x, weight, bias, input_scale, grad_out, out):
    nc = tc.nc
    g_view = grad_out.rearrange("(p a) k -> p a k", a=A)
    o_view = out.rearrange("(p a) n -> p a n", a=A)

    with ExitStack() as ctx:
        const = ctx.enter_context(tc.tile_pool(name="const", bufs=1))
        big = ctx.enter_context(tc.tile_pool(name="big", bufs=8))
        wraw = ctx.enter_context(tc.tile_pool(name="wraw", bufs=1))
        keep = ctx.enter_context(tc.tile_pool(name="keep", bufs=1))
        ggrp = ctx.enter_context(tc.tile_pool(name="ggrp", bufs=3))
        wgrp = ctx.enter_context(tc.tile_pool(name="wgrp", bufs=6))
        psum = ctx.enter_context(tc.psum_pool(name="psum", bufs=1))
        ctx.enter_context(tc.manual_schedule())

        ident = const.tile([P, P], F32, name="ident")
        make_identity(nc, ident[:])

        g_words = {}
        w_src = {}

        def load_g(a0, count):
            t = big.tile([P, count, K], BF16, name="graw%d" % a0, tag="big")
            nc.sync.dma_start(out=t[:], in_=g_view[:, a0 : a0 + count, :])
            for i in range(count):
                g_words[a0 + i] = t[:, i, :].bitcast(F32)

        def load_w(c, n0, nn):
            t = wraw.tile([P, 4, NT * nn], BF16, name="wr%d_%d" % (c, n0))
            for u in range(2):
                r0 = 512 * c + 256 * u
                nc.sync.dma_start(
                    out=t[:, 2 * u : 2 * u + 2, :],
                    in_=weight[r0 : r0 + 256, NT * n0 : NT * (n0 + nn)].rearrange("(q e) w -> q e w", e=2),
                )
            for i in range(nn):
                w_src[(c, n0 + i)] = t[:, :, NT * i : NT * (i + 1)]

        load_w(0, 0, 1)
        load_g(0, 2)
        load_g(2, 2)
        for a in range(4, A):
            load_g(a, 1)
        for c in range(1, C):
            load_w(c, 0, 1)
        for c in range(C):
            load_w(c, 1, 1)
        for c in range(C):
            load_w(c, 2, 2)

        g_grp = {}
        g_codes = {}
        g_scales = {}

        def g_transpose(a, vector_second):
            grp = ggrp.tile([P, C, P, 2], F32, name="ggrp", align_bytes=64)
            g_grp[a] = grp
            for b in range(2):
                bank = 2 + (2 * a + b) % 6
                xt = psum.tile([P, 2, 2, P], F32, name="xt%d_%d" % (a, b), tag="bank%d" % bank)
                for c2 in range(2):
                    for u in range(2):
                        w0 = 256 * (2 * b + c2) + 128 * u
                        nc.tensor.transpose(xt[:, c2, u, :], g_words[a][:, w0 : w0 + 128], ident[:])
                src = xt[:].rearrange("p c u r -> p c r u")
                dst = grp[:, 2 * b : 2 * b + 2, :, :]
                if b == 1 and vector_second:
                    nc.vector.tensor_copy(out=dst, in_=src)
                else:
                    nc.scalar.copy(out=dst, in_=src)

        def g_quantise(a):
            gc = keep.tile([P, C * P], U32, name="gc%d" % a, align_bytes=64)
            gs = keep.tile([P, C * P], U8, name="gs%d" % a, align_bytes=64)
            nc.vector.quantize_mx(
                out=gc[:].bitcast(E5X4),
                scales=gs[:],
                in_=g_grp[a][:].rearrange("p c r u -> p (c r u)").bitcast(BF16),
            )
            g_codes[a] = gc
            g_scales[a] = gs

        w_grp = {}
        w_codes = {}
        w_scales = {}

        def w_regroup(c, n, v_cols):
            src = w_src[(c, n)]
            grp = wgrp.tile([P, NT, 4], BF16, name="wgrp", align_bytes=64)
            w_grp[(c, n)] = grp
            if v_cols > 0:
                nc.vector.tensor_copy(
                    out=grp[:, 0:v_cols, :].rearrange("p (c i) t -> p c t i", i=4),
                    in_=src[:, :, 0:v_cols].rearrange("p t (c i) -> p c t i", i=4),
                )
            if v_cols < NT:
                nc.scalar.copy(
                    out=grp[:, v_cols:NT, :].rearrange("p (c i) t -> p c t i", i=4),
                    in_=src[:, :, v_cols:NT].rearrange("p t (c i) -> p c t i", i=4),
                )

        def w_quantise(c, n):
            wc = keep.tile([P, NT], U32, name="wc%d_%d" % (c, n), align_bytes=64)
            ws = keep.tile([P, NT], U8, name="ws%d_%d" % (c, n), align_bytes=64)
            nc.vector.quantize_mx(
                out=wc[:].bitcast(E4X4),
                scales=ws[:],
                in_=w_grp[(c, n)][:].rearrange("p w t -> p (w t)"),
            )
            w_codes[(c, n)] = wc
            w_scales[(c, n)] = ws

        accs = {}
        out_rows = {}

        def sweep(tiles, n, c):
            for a in tiles:
                if c == 0:
                    accs[(a, n)] = psum.tile([P, NT], F32, name="acc%d_%d" % (a, n), tag="bank%d" % a)
                nc.tensor.matmul_mx(
                    out=accs[(a, n)][:],
                    lhsT=g_codes[a][:, P * c : P * c + P].bitcast(E5X4),
                    lhsT_scale=g_scales[a][:, P * c : P * c + P],
                    rhs=w_codes[(c, n)][:].bitcast(E4X4),
                    rhs_scale=w_scales[(c, n)][:],
                    start=(c == 0),
                    stop=(c == C - 1),
                )

        def evacuate(a, n, lo=0, hi=NT):
            if a not in out_rows:
                out_rows[a] = big.tile([P, IN], F32, name="orow%d" % a, tag="big")
            nc.scalar.copy(out=out_rows[a][:, NT * n + lo : NT * n + hi], in_=accs[(a, n)][:, lo:hi])

        def store(a, lo, hi):
            nc.sync.dma_start(out=o_view[:, a, lo:hi], in_=out_rows[a][:, lo:hi])

        low = [0, 1, 2, 3]
        high = [4, 5, 6, 7]

        def round_of(n):
            sweep(low + high, n, 0)
            sweep(low + high, n, 1)
            for tiles in (low, high):
                sweep(tiles, n, 2)
                sweep(tiles, n, 3)
                for a in tiles:
                    evacuate(a, n)
                    if n == 1:
                        store(a, 0, 2 * NT)
                    if n == 2:
                        store(a, 2 * NT, 3 * NT)

        w_regroup(0, 0, V_COLS)
        w_quantise(0, 0)
        for a in range(6):
            g_transpose(a, a % 2 == 1)
            g_quantise(a)
        g_transpose(6, False)
        g_transpose(7, False)
        g_quantise(6)
        w_regroup(1, 0, V_COLS)
        g_quantise(7)
        w_quantise(1, 0)
        for c, n in ((2, 0), (3, 0), (0, 1), (1, 1)):
            w_regroup(c, n, V_COLS)
            w_quantise(c, n)

        round_of(0)

        w_regroup(2, 1, NT)
        w_regroup(3, 1, NT)
        w_quantise(2, 1)
        w_quantise(3, 1)
        w_regroup(0, 3, 0)
        w_regroup(1, 3, 0)
        w_regroup(0, 2, NT)
        w_regroup(1, 2, NT)
        w_quantise(0, 2)
        w_quantise(0, 3)
        w_regroup(2, 2, NT)
        w_quantise(1, 2)
        w_quantise(1, 3)
        w_regroup(3, 2, NT)
        w_quantise(2, 2)
        w_quantise(3, 2)
        w_regroup(2, 3, NT)
        w_regroup(3, 3, NT)
        w_quantise(2, 3)
        w_quantise(3, 3)

        round_of(1)
        round_of(2)

        for a in range(A):
            for c in range(C):
                sweep([a], 3, c)
            if a < A - 1:
                evacuate(a, 3)
                store(a, 3 * NT, 4 * NT)
        for lo in (0, NT // 2):
            evacuate(7, 3, lo, lo + NT // 2)
            store(7, 3 * NT + lo, 3 * NT + lo + NT // 2)
